import numpy as np
import ml_dtypes


def mxq(x, axis, fmt="e4m3"):
    dtype, down = {"e4m3": (ml_dtypes.float8_e4m3fn, 7), "e5m2": (ml_dtypes.float8_e5m2, 14)}[fmt]
    v = np.moveaxis(np.asarray(x, np.float32).astype(ml_dtypes.bfloat16).astype(np.float64), axis, -1)
    blocks = v.reshape(v.shape[:-1] + (-1, 32))
    amax = np.abs(blocks).max(-1, keepdims=True)
    byte = np.maximum(np.where(amax > 0, np.frexp(amax)[1] - 1 + 127, 0) - down, 1)
    scale = np.exp2(byte - 127.0)
    codes = (blocks / scale).astype(np.float32).astype(dtype).astype(np.float64)
    return np.moveaxis((codes * scale).reshape(v.shape), -1, axis)


WIDE = False


def mx_kscale(k):
    if not WIDE:
        return np.ones(k)
    levels = np.array([18, -18])
    if k % 512:
        return np.exp2(np.random.permutation(np.resize(levels, k // 32))).repeat(32)
    a = np.empty((k // 512, 16))
    for p in range(k // 512):
        a[p, :8] = np.random.permutation(np.resize(levels, 8))
        for g in range(8):
            far = levels[np.abs(levels - a[p, g]) >= 10]
            a[p, g + 8] = far[np.random.randint(len(far))]
    return np.exp2(a.ravel()).repeat(32)


BF16 = ml_dtypes.bfloat16


def bf(x):
    return np.asarray(x, np.float32).astype(BF16)


def f64(x):
    return np.asarray(x).astype(np.float64)


B, T, E, C, XB = 1, 1024, 1024, 1024, 512
SCALE_BASE = float(XB)


def rotate_every_two(z):
    z1 = z[..., ::2]
    z2 = z[..., 1::2]
    return np.stack([-z2, z1], axis=-1).reshape(z.shape)


def xpos_tables():
    dim_scale = (f64(np.arange(0, C, 2)) + 0.4 * C) / (1.4 * C)
    pos = f64(np.arange(T))
    scale = dim_scale[None, :] ** (pos[:, None] / SCALE_BASE)
    inv_freq = 1.0 / (10000.0 ** (f64(np.arange(0, C, 2)) / C))
    sinusoid = pos[:, None] * inv_freq[None, :]
    sin = np.repeat(np.sin(sinusoid) * scale, 2, axis=-1)
    cos = np.repeat(np.cos(sinusoid) * scale, 2, axis=-1)
    return cos, sin


def xpos_back(g):
    cos, sin = xpos_tables()
    return g * cos - rotate_every_two(g) * sin


def setup_inputs():
    s = mx_kscale(T)[:, None]
    uq = mx_kscale(C)
    uk = mx_kscale(C)
    x = bf(np.random.standard_normal((B, T, E)) * s)
    w_q = bf(np.random.standard_normal((E, C)) * 0.5 / np.sqrt(E) / uq)
    w_k = bf(np.random.standard_normal((E, C)) * 0.5 / np.sqrt(E) / uk)
    g0 = bf(4.0 * np.random.standard_normal((B, T, C)) * np.exp2(np.random.randint(-6, 1, (B, T, 1))) / s * uq)
    g1 = bf(4.0 * np.random.standard_normal((B, T, C)) * np.exp2(np.random.randint(-6, 1, (B, T, 1))) / s * uk)
    return {"x": x, "w_q": w_q, "w_k": w_k, "grad_0": g0, "grad_1": g1}


def reference(x, w_q, w_k, grad_0, grad_1):
    xt = f64(x).reshape(B * T, E)
    dq = xpos_back(f64(grad_0).reshape(B * T, C))
    dk = xpos_back(f64(grad_1).reshape(B * T, C))
    dz = np.concatenate([dq, dk], axis=1)
    w = np.concatenate([f64(w_q), f64(w_k)], axis=1)
    dx = mxq(dz, 1, "e5m2") @ mxq(w, 1, "e4m3").T
    dw = mxq(xt, 0, "e4m3").T @ mxq(dz, 0, "e5m2")
    return dx.reshape(B, T, E), dw[:, :C], dw[:, C:]

@@ -1,0 +1,376 @@
+import math
+from contextlib import ExitStack
+
+import concourse.mybir as mybir
+from concourse.masks import make_identity
+
+F32 = mybir.dt.float32
+BF16 = mybir.dt.bfloat16
+U32 = mybir.dt.uint32
+I32 = mybir.dt.int32
+U8 = mybir.dt.uint8
+E4M3 = mybir.dt.float8_e4m3fn_x4
+E5M2 = mybir.dt.float8_e5m2_x4
+ALU = mybir.AluOpType
+ACT = mybir.ActivationFunctionType
+
+P = 128
+T, E, C = 1024, 1024, 1024
+XPOS_BASE = 512.0
+N = P + 3
+
+FLOPS = 2 * 2 * T * E * 2 * C
+
+CHUNKS = [(0, 0, 0), (0, 1, 0), (1, 0, 0), (1, 1, 0), (0, 0, 1), (1, 0, 1), (0, 1, 1), (1, 1, 1)]
+STAGE = 8
+MXHALF = 10
+LEVELS = [(0, 128, 128), (0, 256, 256), (0, 512, 512)]
+LOADS = [('g',0,0,0),('w',0,0),('g',0,1,0),('w',1,0),('g',1,0,0),('w',0,1),('g',1,1,0),('w',1,1),('x',0),('g',0,0,1),('x',1),('g',1,0,1),('g',0,1,1),('g',1,1,1)]
+TABLE = [(2,0,0),(3,0,0),(2,1,1),(3,1,1),(0,2,5),(1,2,6),(2,2,9),(3,2,10)]
+WS = 0
+XS = 5
+GTOK = 192
+FAST = 0
+VK = (15,)
+
+
+def tile_multiscaleretention_pa_v_kernel(tc, x, w_q, w_k, grad_0, grad_1, out_0, out_1, out_2):
+    nc = tc.nc
+    x_hbm = x[0].rearrange("(g p j) e -> p g j e", g=2, j=4)
+    g_hbm = [g[0].rearrange("(g p j) e -> p g j e", g=2, j=4) for g in (grad_0, grad_1)]
+    w_hbm = [w.rearrange("(h t p) c -> p h t c", h=2, t=4) for w in (w_q, w_k)]
+    dx_hbm = out_0[0].rearrange("(g p j) e -> p g j e", g=2, j=4)
+    dw_hbm = [out_1, out_2]
+
+    with ExitStack() as ctx:
+        keep = ctx.enter_context(tc.tile_pool(name="keep", bufs=1))
+        psum = ctx.enter_context(tc.psum_pool(name="psum", bufs=2))
+        raw = ctx.enter_context(tc.tile_pool(name="raw", bufs=3))
+
+        graw, xraw, wraw = {}, {}, {}
+
+        def load_g(a, g, tg):
+            t = raw.tile([P, 4, 512], BF16, tag="graw", name="graw", align_bytes=64, bufs=5)
+            nc.sync.dma_start(out=t[:], in_=g_hbm[a][:, tg, :, 512 * g : 512 * (g + 1)])
+            graw[a, g, tg] = t
+
+        def load_x(tg):
+            t = raw.tile([P, 4, E], BF16, tag="raw", name="xraw", align_bytes=64, bufs=3)
+            nc.sync.dma_start(out=t[:], in_=x_hbm[:, tg])
+            xraw[tg] = t
+
+        def load_w(a, h):
+            t = raw.tile([P, 4, C], BF16, tag="raw", name="wraw", align_bytes=64, bufs=3)
+            nc.sync.dma_start(out=t[:], in_=w_hbm[a][:, h])
+            wraw[a, h] = t
+
+
+        tab = keep.tile([P, 4, 2, T], F32)
+        zk = keep.tile([P, 4, 3, 3], F32)
+        seed = ctx.enter_context(tc.tile_pool(name="seed", bufs=1))
+        tt = seed.tile([P, N], F32)
+        jj = seed.tile([P, 4], F32)
+        nc.gpsimd.iota(jj[:].rearrange("p (g u) -> p g u", u=2), pattern=[[256, 2], [1, 2]], base=0, channel_multiplier=2, allow_small_or_imprecise_dtypes=True)
+        tenk = seed.tile([P, 4], F32)
+        nc.vector.memset(tenk[:], 10000.0)
+        ex = seed.tile([P, 4], F32)
+        nc.gpsimd.tensor_scalar(out=ex[:], in0=jj[:], scalar1=-2.0 / C, scalar2=0.0, op0=ALU.mult, op1=ALU.add)
+        ww = seed.tile([P, 4], F32)
+        nc.gpsimd.tensor_tensor(out=ww[:], in0=tenk[:], in1=ex[:], op=ALU.pow)
+        nc.gpsimd.iota(tt[:, 0:P], pattern=[[4, P]], base=0, channel_multiplier=0, allow_small_or_imprecise_dtypes=True)
+        for k, v in enumerate((1.0, 2.0, 512.0)):
+            nc.vector.memset(tt[:, P + k : P + k + 1], v)
+        ident = keep.tile([P, P], F32)
+        make_identity(nc, ident[:])
+        dd = seed.tile([P, 4], F32)
+        nc.vector.tensor_scalar(out=dd[:], in0=jj[:], scalar1=2.0 / (1.4 * C), scalar2=0.4 / 1.4, op0=ALU.mult, op1=ALU.add)
+        lnd = seed.tile([P, 4], F32)
+        nc.scalar.activation(out=lnd[:], in_=dd[:], func=ACT.Ln)
+        lnr = seed.tile([P, 4], F32)
+        nc.vector.tensor_scalar(out=lnr[:], in0=lnd[:], scalar1=1.0 / XPOS_BASE, scalar2=None, op0=ALU.mult)
+        rr = seed.tile([P, 4, N], F32)
+        for k in range(4):
+            nc.scalar.activation(out=rr[:, k, :], in_=tt[:], func=ACT.Exp, scale=lnr[:, k : k + 1])
+
+        sd = {}
+
+        def seeds_phase(g):
+            gs = slice(2 * g, 2 * g + 2)
+            turns = seed.tile([P, 2, N], F32, name="turns%d" % g)
+            nc.vector.scalar_tensor_tensor(
+                out=turns[:], in0=tt[:].unsqueeze(1).to_broadcast([P, 2, N]), scalar=1.0 / (2.0 * math.pi),
+                in1=ww[:, gs].unsqueeze(2).to_broadcast([P, 2, N]), op0=ALU.mult, op1=ALU.mult)
+            whole = seed.tile([P, 2, N], I32, name="whole%d" % g)
+            nc.vector.tensor_copy(out=whole[:], in_=turns[:])
+            frac = seed.tile([P, 2, N], F32, name="frac%d" % g)
+            nc.vector.tensor_tensor(out=frac[:], in0=turns[:], in1=whole[:], op=ALU.subtract)
+            wrap = seed.tile([P, 2, N], F32, name="wrap%d" % g)
+            nc.vector.scalar_tensor_tensor(out=wrap[:], in0=frac[:], scalar=0.25, in1=frac[:], op0=ALU.is_gt, op1=ALU.subtract)
+            sd[g] = frac, wrap
+
+        def seeds_sin(g):
+            gs = slice(2 * g, 2 * g + 2)
+            frac, wrap = sd[g]
+            cs = seed.tile([P, 2, N], F32, name="cs%d" % g)
+            nc.scalar.activation(out=cs[:], in_=wrap[:], func=ACT.Sin, scale=-2.0 * math.pi, bias=0.5 * math.pi)
+            sn = seed.tile([P, 2, N], F32, name="sn%d" % g)
+            nc.scalar.activation(out=sn[:], in_=frac[:], func=ACT.Sin, scale=2.0 * math.pi)
+            for k, f in ((0, cs), (1, sn)):
+                nc.vector.tensor_tensor(out=zk[:, gs, k, :], in0=f[:, :, P:N], in1=rr[:, gs, P:N], op=ALU.mult)
+            for k, f in ((0, cs), (1, sn)):
+                nc.vector.tensor_tensor(out=tab[:, gs, k, 0:P], in0=f[:, :, 0:P], in1=rr[:, gs, 0:P], op=ALU.mult)
+            nc.vector.tensor_scalar(out=zk[:, gs, 2, :], in0=zk[:, gs, 1, :], scalar1=-1.0, scalar2=None, op0=ALU.mult)
+
+        prod = ctx.enter_context(tc.tile_pool(name="prod", bufs=2))
+        dpool = ctx.enter_context(tc.tile_pool(name="dpool", bufs=3))
+        stage = ctx.enter_context(tc.tile_pool(name="stage", bufs=STAGE))
+
+        tmps = {}
+
+        def level_s(gu, k):
+            src, dst, n = LEVELS[k]
+            tmp = prod.tile([P, 2, 512], F32, tag="tmp", name="tmp", align_bytes=64)
+            tmps[gu, k] = tmp
+            for b in range(2):
+                nc.scalar.activation(out=tmp[:, b, 0:n], in_=tab[:, gu, 1 - b, src : src + n], func=ACT.Copy, scale=zk[:, gu, 2 - b, k : k + 1])
+
+        def level_v(gu, k):
+            src, dst, n = LEVELS[k]
+            nc.vector.scalar_tensor_tensor(
+                out=tab[:, gu, :, dst : dst + n], in0=tab[:, gu, :, src : src + n], scalar=zk[:, gu, 0, k : k + 1],
+                in1=tmps[gu, k][:, :, 0:n], op0=ALU.mult, op1=ALU.add)
+
+        xc = keep.tile([P, 2, E], U32, align_bytes=64)
+        xs = keep.tile([P, 2, E], U8, align_bytes=64)
+        wc, ws, fc, fs = {}, {}, {}, {}
+        for a in range(2):
+            for g in range(2):
+                for d, nm, dt in ((wc, "wc", U32), (ws, "ws", U8), (fc, "fc", U32), (fs, "fs", U8)):
+                    t = keep.tile([P, 1024], dt, name="%s%d%d" % (nm, a, g), align_bytes=64)
+                    d[a, g] = t
+        kc, ks = {}, {}
+        for a in range(2):
+            for d, nm, dt in ((kc, "kc", U32), (ks, "ks", U8)):
+                t = keep.tile([P, 2, C], dt, name="%s%d" % (nm, a), align_bytes=64)
+                d[a] = t
+
+        dfeat, dtok, gts, pqs = {}, {}, {}, {}
+
+        def g_turn(k):
+            i, h = divmod(k, 2)
+            a, g, tg = CHUNKS[i]
+            gt = psum.tile([P, 512], F32, tag="gt", name="gt")
+            gts[k] = gt
+            gw = graw[a, g, tg][:].bitcast(F32)
+            for u in range(2):
+                for jx in range(2):
+                    o = (2 * u + jx) * P
+                    nc.tensor.transpose(gt[:, o : o + P], gw[:, 2 * h + jx, u : 256 : 2], ident[:])
+
+        def gview(k):
+            i, h = divmod(k, 2)
+            a, g, tg = CHUNKS[i]
+            c0 = 512 * tg + 256 * h
+            gv = gts[k][:].bitcast(BF16).rearrange("p (u k e) -> p u k e", u=2, e=2)
+            return gv, tab[:, 2 * g : 2 * g + 2, :, c0 : c0 + 256]
+
+        def prod_cos(k):
+            gv, tb = gview(k)
+            pp = prod.tile([P, 2, 512], F32, tag="pp", name="pp", align_bytes=64)
+            qq = prod.tile([P, 2, 512], F32, tag="qq", name="qq", align_bytes=64)
+            pqs[k] = pp, qq
+            cb = tb[:, :, 0, :].unsqueeze(3).to_broadcast([P, 2, 256, 2])
+            nc.vector.tensor_tensor(out=pp[:].rearrange("p u (k e) -> p u k e", e=2), in0=gv, in1=cb, op=ALU.mult)
+
+        def prod_sin(k, e, u=None):
+            gv, tb = gview(k)
+            us = slice(0, 2) if u is None else slice(u, u + 1)
+            nc.vector.scalar_tensor_tensor(
+                out=pqs[k][1][:, e, :].rearrange("p (u k) -> p u k", u=2)[:, us], in0=gv[:, us, :, 1 - e],
+                scalar=1.0 - 2.0 * e, in1=tb[:, us, 1, :], op0=ALU.mult, op1=ALU.mult)
+
+        def add(k, engine, lo, hi):
+            i, h = divmod(k, 2)
+            if i not in dfeat:
+                d = dpool.tile([P, 2048], BF16, tag="dfeat", name="dfeat", align_bytes=64)
+                dfeat[i] = d
+            pp, qq = pqs[k]
+            o = 1024 * h
+            engine.tensor_tensor(
+                out=dfeat[i][:, o + 4 * lo : o + 4 * hi].rearrange("p (k u e) -> p k u e", u=2, e=2),
+                in0=pp[:].rearrange("p u (k e) -> p k u e", e=2)[:, lo:hi],
+                in1=qq[:].rearrange("p e (u k) -> p k u e", u=2)[:, lo:hi], op=ALU.add)
+
+        def quant_feat(i, lo=0, hi=2):
+            a, g, tg = CHUNKS[i]
+            cols = slice(512 * tg + 256 * lo, 512 * tg + 256 * hi)
+            nc.vector.quantize_mx(out=fc[a, g][:, cols].bitcast(E5M2), scales=fs[a, g][:, cols], in_=dfeat[i][:, 1024 * lo : 1024 * hi])
+
+        def d_turn(i, u, eng="S"):
+            if i not in dtok:
+                d = dpool.tile([P, 2048], BF16, tag="dtok", name="dtok", align_bytes=64, bufs=2)
+                dtok[i] = d
+            dw = dfeat[i][:].bitcast(F32)
+            dv = dtok[i][:].rearrange("q (p u r) -> q u p r", u=2, r=8)[:, u].rearrange("q p (e j) -> q p e j", j=4)
+            dt = psum.tile([P, 512], F32, tag="dt", name="dt")
+            for j in range(4):
+                nc.tensor.transpose(dt[:, P * j : P * (j + 1)], dw[:, 256 * j + u : 256 * (j + 1) : 2], ident[:])
+            cp = nc.scalar.copy if eng == "S" else nc.vector.tensor_copy
+            cp(out=dv, in_=dt[:].bitcast(BF16).rearrange("q (j p e) -> q p e j", j=4, e=2))
+
+        def quant_tok(i):
+            a, g, tg = CHUNKS[i]
+            cols = slice(512 * g, 512 * (g + 1))
+            nc.vector.quantize_mx(out=kc[a][:, tg, cols].bitcast(E5M2), scales=ks[a][:, tg, cols], in_=dtok[i][:])
+
+        wide = {}
+
+        def wide_tile(key):
+            if key not in wide:
+                t = dpool.tile([P, 2048], BF16, tag="wide", name="wide", align_bytes=64, bufs=3)
+                wide[key] = t
+            return wide[key]
+
+        def x_lay(tg, h, eng):
+            cp = nc.scalar.copy if eng == "S" else nc.vector.tensor_copy
+            cp(out=wide_tile(("x", tg, h))[:].rearrange("p (e j) -> p e j", j=4), in_=xraw[tg][:, :, 512 * h : 512 * (h + 1)].rearrange("p j e -> p e j"))
+
+        def x_quant(tg, h):
+            cols = slice(512 * h, 512 * (h + 1))
+            nc.vector.quantize_mx(out=xc[:, tg, cols].bitcast(E4M3), scales=xs[:, tg, cols], in_=wide["x", tg, h][:])
+
+        def w_turn(a, h, g, b, eng):
+            wv = wraw[a, h][:].bitcast(F32)
+            ov = wide_tile((a, h, g))[:].bitcast(F32)
+            wt = psum.tile([P, 512], F32, tag="acc", name="wt", bufs=4)
+            for u in range(2):
+                for k in range(2):
+                    o = (2 * u + k) * P
+                    nc.tensor.transpose(wt[:, o : o + P], wv[:, 2 * b + k, 256 * g + u : 256 * (g + 1) : 2], ident[:])
+            cp = nc.scalar.copy if eng == "S" else nc.vector.tensor_copy
+            cp(out=ov[:, 512 * b : 512 * (b + 1)].rearrange("p (n u) -> p n u", u=2), in_=wt[:].rearrange("p (u n) -> p n u", u=2))
+
+        def w_quant(a, h, g):
+            cols = slice(512 * h, 512 * (h + 1))
+            nc.vector.quantize_mx(out=wc[a, g][:, cols].bitcast(E4M3), scales=ws[a, g][:, cols], in_=wide[a, h, g][:])
+
+        def leave(acc, dst, eng):
+            o = stage.tile([P, 512], F32, tag="o", name="o", align_bytes=64)
+            cp = nc.scalar.copy if eng == "S" else nc.vector.tensor_copy
+            cp(out=o[:], in_=acc[:])
+            nc.sync.dma_start(out=dst, in_=o[:])
+
+        def dw_mm(a, g, eb):
+            acc = psum.tile([P, 512], F32, tag="acc", name="acc", bufs=4)
+            m = slice(P * eb, P * (eb + 1))
+            n = slice(512 * g, 512 * (g + 1))
+            for tg in range(2):
+                nc.tensor.matmul_mx(
+                    out=acc[:], lhsT=xc[:, tg, m].bitcast(E4M3), lhsT_scale=xs[:, tg, m],
+                    rhs=kc[a][:, tg, n].bitcast(E5M2), rhs_scale=ks[a][:, tg, n], start=(tg == 0), stop=(tg == 1))
+            return acc, dw_hbm[a][m, n]
+
+        def dx_mm(tg, j, h):
+            acc = psum.tile([P, 512], F32, tag="acc", name="acc", bufs=4)
+            m = slice(512 * tg + P * j, 512 * tg + P * (j + 1))
+            n = slice(512 * h, 512 * (h + 1))
+            for s, (a, g) in enumerate([(0, 0), (0, 1), (1, 0), (1, 1)]):
+                nc.tensor.matmul_mx(
+                    out=acc[:], lhsT=fc[a, g][:, m].bitcast(E5M2), lhsT_scale=fs[a, g][:, m],
+                    rhs=wc[a, g][:, n].bitcast(E4M3), rhs_scale=ws[a, g][:, n], start=(s == 0), stop=(s == 3))
+            return acc, dx_hbm[:, tg, j, n]
+
+        ctx.enter_context(tc.manual_schedule())
+        V, G = nc.vector, nc.gpsimd
+        at = CHUNKS.index
+        for what in LOADS:
+            (load_g if what[0] == "g" else load_x if what[0] == "x" else load_w)(*what[1:])
+        seeds_phase(0)
+        seeds_phase(1)
+        seeds_sin(0)
+        g_turn(0)
+        for k in range(2):
+            for u in range(2):
+                level_s(u, k)
+                level_v(u, k)
+        seeds_sin(1)
+        w_units = [(a, h, g) for h in range(2) for a in range(2) for g in range(2)]
+        x_units = [(tg, h) for tg in range(2) for h in range(2)]
+        L = {k: [] for k in range(-1, 17)}
+        S_ = {k: [] for k in range(-1, 17)}
+        for gu, k, when in TABLE:
+            S_[when - 1].append((gu, k))
+            L[when].append(lambda gu=gu, k=k: level_v(gu, k))
+        for gu, k in S_[-1]:
+            level_s(gu, k)
+        for n, u in enumerate(x_units):
+            L[XS + n + 1].append(lambda u=u: x_quant(*u))
+        for n, u in enumerate(w_units):
+            L[WS + n + 1].append(lambda u=u: w_quant(*u))
+        mx = []
+        for a in range(2):
+            for g in range(2):
+                i = max(at((a, g, tg)) for tg in range(2))
+                mx.append((2 * i + 4 - FAST, 0, [lambda a=a, g=g, e=e: dw_mm(a, g, e) for e in range(8)]))
+        for tg in range(2):
+            i = max(at((a, g, tg)) for a in range(2) for g in range(2))
+            mx.append((2 * i + 3, 1, [lambda tg=tg, j=j, h=h: dx_mm(tg, j, h) for j in range(4) for h in range(2)]))
+        mx.sort(key=lambda m: (m[0], m[1]))
+        mx = [(av, 4 if kind else 2, f) for av, kind, fs_ in mx for f in fs_]
+        cnt = 0
+        for k in range(16):
+            i = k // 2
+            if k + 1 < 16:
+                g_turn(k + 1)
+            n = 0
+            exits = []
+            while mx and mx[0][0] <= k and n + mx[0][1] <= MXHALF:
+                n += mx[0][1]
+                if len(exits) == 3:
+                    leave(*exits.pop(0), "S")
+                exits.append(mx.pop(0)[2]())
+            for acc, dst in exits:
+                leave(acc, dst, "S")
+            if k % 2 == 0 and i >= 1 and FAST:
+                d_turn(i - 1, 0)
+            prod_cos(k)
+            prod_sin(k, 0)
+            if k >= 1 and GTOK < 256 and k - 1 not in VK:
+                add(k - 1, V, GTOK, 256)
+            if k % 2 == 0 and i >= 1:
+                quant_feat(i - 1)
+                if not FAST:
+                    d_turn(i - 1, 0)
+                d_turn(i - 1, 1)
+            if WS <= k < WS + 8:
+                a, h, g = w_units[k - WS]
+                w_turn(a, h, g, 0, "S")
+                w_turn(a, h, g, 1, "S")
+            if k % 2 == 1 and i >= 1:
+                quant_tok(i - 1)
+            if XS <= k < XS + 4:
+                tg, h = x_units[k - XS]
+                x_lay(tg, h, "S")
+            for f in L[k]:
+                f()
+            for gu, kk in S_[k]:
+                level_s(gu, kk)
+            if k == 15:
+                quant_feat(7, 0, 1)
+            prod_sin(k, 1, 0)
+            prod_sin(k, 1, 1)
+            if k in VK:
+                add(k, V, 0, 256)
+            elif GTOK > 0:
+                add(k, G, 0, GTOK)
+        d_turn(7, 0, "S")
+        d_turn(7, 1, "V")
+        quant_feat(7, 1, 2)
+        last = [m for m in mx if m[0] > 17]
+        mx = [m for m in mx if m[0] <= 17]
+        while mx or last:
+            acc, dst = (mx or last).pop(0)[2]()
+            leave(acc, dst, "SV"[cnt % 2])
+            cnt += 1
+            if cnt == 4:
+                quant_tok(7)

@@ -21,16 +21,19 @@ N = P + 3
 
 FLOPS = 2 * 2 * T * E * 2 * C
 
-CHUNKS = [(0, 0, 0), (0, 1, 0), (1, 0, 0), (1, 1, 0), (0, 0, 1), (1, 0, 1), (0, 1, 1), (1, 1, 1)]
+CELLS = [(0, 0, 0), (0, 1, 0), (1, 0, 0), (1, 1, 0), (0, 0, 1), (0, 0, 2), (0, 0, 3), (0, 1, 1), (1, 0, 1), (1, 1, 1), (0, 1, 2), (0, 1, 3), (1, 0, 2), (1, 1, 2), (1, 0, 3), (1, 1, 3)]
 STAGE = 8
-MXHALF = 10
+MXA = 4
+MXB = 8
 LEVELS = [(0, 128, 128), (0, 256, 256), (0, 512, 512)]
-LOADS = [('g',0,0,0),('w',0,0),('g',0,1,0),('w',1,0),('g',1,0,0),('w',0,1),('g',1,1,0),('w',1,1),('x',0),('g',0,0,1),('x',1),('g',1,0,1),('g',0,1,1),('g',1,1,1)]
-TABLE = [(2,0,0),(3,0,0),(2,1,1),(3,1,1),(0,2,5),(1,2,6),(2,2,9),(3,2,10)]
-WS = 0
-XS = 5
-GTOK = 192
-FAST = 0
+GBUFS = 6
+DFEAT = 6
+QCUT = 256
+LOADS = [("g", 0, 0, 0), ("w",0,0), ("g", 0, 1, 0), ("w",1,0), ("g", 1, 0, 0), ("g", 1, 1, 0), ("x",0), ("g", 0, 0, 1), ("w",0,1), ("g", 0, 0, 2), ("g", 0, 0, 3), ("x",1), ("g", 0, 1, 1), ("g", 1, 0, 1), ("w",1,1), ("g", 1, 1, 1), ("g", 0, 1, 2), ("g", 0, 1, 3), ("g", 1, 0, 2), ("g", 1, 1, 2), ("g", 1, 0, 3), ("g", 1, 1, 3)]
+TABLE = [(0,0,-1),(1,0,-1),(2,0,0),(3,0,0),(0,1,1),(1,1,1),(0,2,3),(1,2,4),(2,1,5),(3,1,5),(2,2,7),(3,2,8)]
+WS = [0, 1, 2, 3, 6, 7, 8, 9]
+XS = 3
+GTOK = 0
 VK = (15,)
 
 
@@ -47,79 +50,88 @@ def tile_multiscaleretention_pa_v_kernel(tc, x, w_q, w_k, grad_0, grad_1, out_0,
         psum = ctx.enter_context(tc.psum_pool(name="psum", bufs=2))
         raw = ctx.enter_context(tc.tile_pool(name="raw", bufs=3))
 
+        ctx.enter_context(tc.manual_schedule())
         graw, xraw, wraw = {}, {}, {}
 
-        def load_g(a, g, tg):
-            t = raw.tile([P, 4, 512], BF16, tag="graw", name="graw", align_bytes=64, bufs=5)
-            nc.sync.dma_start(out=t[:], in_=g_hbm[a][:, tg, :, 512 * g : 512 * (g + 1)])
-            graw[a, g, tg] = t
+        def load_g(a, g, r):
+            tg, h = divmod(r, 2)
+            t = raw.tile([P, 2, 512], BF16, tag="graw", name="graw", align_bytes=64, bufs=GBUFS)
+            nc.sync.dma_start(out=t[:], in_=g_hbm[a][:, tg, 2 * h : 2 * h + 2, 512 * g : 512 * (g + 1)])
+            graw[a, g, r] = t
 
         def load_x(tg):
-            t = raw.tile([P, 4, E], BF16, tag="raw", name="xraw", align_bytes=64, bufs=3)
+            t = raw.tile([P, 4, E], BF16, tag="xraw", name="xraw", align_bytes=64, bufs=2)
             nc.sync.dma_start(out=t[:], in_=x_hbm[:, tg])
             xraw[tg] = t
 
         def load_w(a, h):
-            t = raw.tile([P, 4, C], BF16, tag="raw", name="wraw", align_bytes=64, bufs=3)
+            t = raw.tile([P, 4, C], BF16, tag="wraw", name="wraw", align_bytes=64, bufs=3)
             nc.sync.dma_start(out=t[:], in_=w_hbm[a][:, h])
             wraw[a, h] = t
 
 
         tab = keep.tile([P, 4, 2, T], F32)
         zk = keep.tile([P, 4, 3, 3], F32)
-        seed = ctx.enter_context(tc.tile_pool(name="seed", bufs=1))
-        tt = seed.tile([P, N], F32)
-        jj = seed.tile([P, 4], F32)
-        nc.gpsimd.iota(jj[:].rearrange("p (g u) -> p g u", u=2), pattern=[[256, 2], [1, 2]], base=0, channel_multiplier=2, allow_small_or_imprecise_dtypes=True)
-        tenk = seed.tile([P, 4], F32)
-        nc.vector.memset(tenk[:], 10000.0)
-        ex = seed.tile([P, 4], F32)
-        nc.gpsimd.tensor_scalar(out=ex[:], in0=jj[:], scalar1=-2.0 / C, scalar2=0.0, op0=ALU.mult, op1=ALU.add)
-        ww = seed.tile([P, 4], F32)
-        nc.gpsimd.tensor_tensor(out=ww[:], in0=tenk[:], in1=ex[:], op=ALU.pow)
-        nc.gpsimd.iota(tt[:, 0:P], pattern=[[4, P]], base=0, channel_multiplier=0, allow_small_or_imprecise_dtypes=True)
-        for k, v in enumerate((1.0, 2.0, 512.0)):
-            nc.vector.memset(tt[:, P + k : P + k + 1], v)
-        ident = keep.tile([P, P], F32)
-        make_identity(nc, ident[:])
-        dd = seed.tile([P, 4], F32)
-        nc.vector.tensor_scalar(out=dd[:], in0=jj[:], scalar1=2.0 / (1.4 * C), scalar2=0.4 / 1.4, op0=ALU.mult, op1=ALU.add)
-        lnd = seed.tile([P, 4], F32)
-        nc.scalar.activation(out=lnd[:], in_=dd[:], func=ACT.Ln)
-        lnr = seed.tile([P, 4], F32)
-        nc.vector.tensor_scalar(out=lnr[:], in0=lnd[:], scalar1=1.0 / XPOS_BASE, scalar2=None, op0=ALU.mult)
-        rr = seed.tile([P, 4, N], F32)
-        for k in range(4):
-            nc.scalar.activation(out=rr[:, k, :], in_=tt[:], func=ACT.Exp, scale=lnr[:, k : k + 1])
+        with tc.tile_pool(name="seed", bufs=1) as seed:
+            tt = seed.tile([P, N], F32)
+            jj = seed.tile([P, 4], F32)
+            nc.gpsimd.iota(jj[:].rearrange("p (g u) -> p g u", u=2), pattern=[[256, 2], [1, 2]], base=0, channel_multiplier=2, allow_small_or_imprecise_dtypes=True)
+            tenk = seed.tile([P, 4], F32)
+            nc.vector.memset(tenk[:], 10000.0)
+            ex = seed.tile([P, 4], F32)
+            nc.gpsimd.tensor_scalar(out=ex[:], in0=jj[:], scalar1=-2.0 / C, scalar2=0.0, op0=ALU.mult, op1=ALU.add)
+            ww = seed.tile([P, 4], F32)
+            nc.gpsimd.tensor_tensor(out=ww[:], in0=tenk[:], in1=ex[:], op=ALU.pow)
+            nc.gpsimd.iota(tt[:, 0:P], pattern=[[4, P]], base=0, channel_multiplier=0, allow_small_or_imprecise_dtypes=True)
+            for k, v in enumerate((1.0, 2.0, 512.0)):
+                nc.vector.memset(tt[:, P + k : P + k + 1], v)
+            ident = keep.tile([P, P], F32)
+            make_identity(nc, ident[:])
+            dd = seed.tile([P, 4], F32)
+            nc.vector.tensor_scalar(out=dd[:], in0=jj[:], scalar1=2.0 / (1.4 * C), scalar2=0.4 / 1.4, op0=ALU.mult, op1=ALU.add)
+            lnd = seed.tile([P, 4], F32)
+            nc.scalar.activation(out=lnd[:], in_=dd[:], func=ACT.Ln)
+            lnr = seed.tile([P, 4], F32)
+            nc.vector.tensor_scalar(out=lnr[:], in0=lnd[:], scalar1=1.0 / XPOS_BASE, scalar2=None, op0=ALU.mult)
+            rr = seed.tile([P, 4, N], F32)
+            for k in range(4):
+                nc.scalar.activation(out=rr[:, k, :], in_=tt[:], func=ACT.Exp, scale=lnr[:, k : k + 1])
 
-        sd = {}
+            sd = {}
 
-        def seeds_phase(g):
-            gs = slice(2 * g, 2 * g + 2)
-            turns = seed.tile([P, 2, N], F32, name="turns%d" % g)
-            nc.vector.scalar_tensor_tensor(
-                out=turns[:], in0=tt[:].unsqueeze(1).to_broadcast([P, 2, N]), scalar=1.0 / (2.0 * math.pi),
-                in1=ww[:, gs].unsqueeze(2).to_broadcast([P, 2, N]), op0=ALU.mult, op1=ALU.mult)
-            whole = seed.tile([P, 2, N], I32, name="whole%d" % g)
-            nc.vector.tensor_copy(out=whole[:], in_=turns[:])
-            frac = seed.tile([P, 2, N], F32, name="frac%d" % g)
-            nc.vector.tensor_tensor(out=frac[:], in0=turns[:], in1=whole[:], op=ALU.subtract)
-            wrap = seed.tile([P, 2, N], F32, name="wrap%d" % g)
-            nc.vector.scalar_tensor_tensor(out=wrap[:], in0=frac[:], scalar=0.25, in1=frac[:], op0=ALU.is_gt, op1=ALU.subtract)
-            sd[g] = frac, wrap
+            def seeds_phase(g):
+                gs = slice(2 * g, 2 * g + 2)
+                turns = seed.tile([P, 2, N], F32, name="turns%d" % g)
+                nc.vector.scalar_tensor_tensor(
+                    out=turns[:], in0=tt[:].unsqueeze(1).to_broadcast([P, 2, N]), scalar=1.0 / (2.0 * math.pi),
+                    in1=ww[:, gs].unsqueeze(2).to_broadcast([P, 2, N]), op0=ALU.mult, op1=ALU.mult)
+                whole = seed.tile([P, 2, N], I32, name="whole%d" % g)
+                nc.vector.tensor_copy(out=whole[:], in_=turns[:])
+                frac = seed.tile([P, 2, N], F32, name="frac%d" % g)
+                nc.vector.tensor_tensor(out=frac[:], in0=turns[:], in1=whole[:], op=ALU.subtract)
+                wrap = seed.tile([P, 2, N], F32, name="wrap%d" % g)
+                nc.vector.scalar_tensor_tensor(out=wrap[:], in0=frac[:], scalar=0.25, in1=frac[:], op0=ALU.is_gt, op1=ALU.subtract)
+                sd[g] = frac, wrap
 
-        def seeds_sin(g):
-            gs = slice(2 * g, 2 * g + 2)
-            frac, wrap = sd[g]
-            cs = seed.tile([P, 2, N], F32, name="cs%d" % g)
-            nc.scalar.activation(out=cs[:], in_=wrap[:], func=ACT.Sin, scale=-2.0 * math.pi, bias=0.5 * math.pi)
-            sn = seed.tile([P, 2, N], F32, name="sn%d" % g)
-            nc.scalar.activation(out=sn[:], in_=frac[:], func=ACT.Sin, scale=2.0 * math.pi)
-            for k, f in ((0, cs), (1, sn)):
-                nc.vector.tensor_tensor(out=zk[:, gs, k, :], in0=f[:, :, P:N], in1=rr[:, gs, P:N], op=ALU.mult)
-            for k, f in ((0, cs), (1, sn)):
-                nc.vector.tensor_tensor(out=tab[:, gs, k, 0:P], in0=f[:, :, 0:P], in1=rr[:, gs, 0:P], op=ALU.mult)
-            nc.vector.tensor_scalar(out=zk[:, gs, 2, :], in0=zk[:, gs, 1, :], scalar1=-1.0, scalar2=None, op0=ALU.mult)
+            def seeds_sin(g):
+                gs = slice(2 * g, 2 * g + 2)
+                frac, wrap = sd[g]
+                cs = seed.tile([P, 2, N], F32, name="cs%d" % g)
+                nc.scalar.activation(out=cs[:], in_=wrap[:], func=ACT.Sin, scale=-2.0 * math.pi, bias=0.5 * math.pi)
+                sn = seed.tile([P, 2, N], F32, name="sn%d" % g)
+                nc.scalar.activation(out=sn[:], in_=frac[:], func=ACT.Sin, scale=2.0 * math.pi)
+                for k, f in ((0, cs), (1, sn)):
+                    nc.vector.tensor_tensor(out=zk[:, gs, k, :], in0=f[:, :, P:N], in1=rr[:, gs, P:N], op=ALU.mult)
+                for k, f in ((0, cs), (1, sn)):
+                    nc.vector.tensor_tensor(out=tab[:, gs, k, 0:P], in0=f[:, :, 0:P], in1=rr[:, gs, 0:P], op=ALU.mult)
+                nc.vector.tensor_scalar(out=zk[:, gs, 2, :], in0=zk[:, gs, 1, :], scalar1=-1.0, scalar2=None, op0=ALU.mult)
+
+            for what in LOADS:
+                (load_g if what[0] == "g" else load_x if what[0] == "x" else load_w)(*what[1:])
+            seeds_phase(0)
+            seeds_phase(1)
+            seeds_sin(0)
+            seeds_sin(1)
 
         prod = ctx.enter_context(tc.tile_pool(name="prod", bufs=2))
         dpool = ctx.enter_context(tc.tile_pool(name="dpool", bufs=3))
@@ -149,62 +161,64 @@ def tile_multiscaleretention_pa_v_kernel(tc, x, w_q, w_k, grad_0, grad_1, out_0,
                     t = keep.tile([P, 1024], dt, name="%s%d%d" % (nm, a, g), align_bytes=64)
                     d[a, g] = t
         kc, ks = {}, {}
-        for a in range(2):
-            for d, nm, dt in ((kc, "kc", U32), (ks, "ks", U8)):
-                t = keep.tile([P, 2, C], dt, name="%s%d" % (nm, a), align_bytes=64)
-                d[a] = t
+
+        def tok_codes(f):
+            if f not in kc:
+                for d, nm, dt in ((kc, "kc", U32), (ks, "ks", U8)):
+                    t = dpool.tile([P, 2, 512], dt, tag=nm, name=nm, align_bytes=64, bufs=3)
+                    d[f] = t
+            return kc[f], ks[f]
 
         dfeat, dtok, gts, pqs = {}, {}, {}, {}
 
         def g_turn(k):
-            i, h = divmod(k, 2)
-            a, g, tg = CHUNKS[i]
+            a, g, r = CELLS[k]
             gt = psum.tile([P, 512], F32, tag="gt", name="gt")
             gts[k] = gt
-            gw = graw[a, g, tg][:].bitcast(F32)
+            gw = graw[a, g, r][:].bitcast(F32)
             for u in range(2):
                 for jx in range(2):
                     o = (2 * u + jx) * P
-                    nc.tensor.transpose(gt[:, o : o + P], gw[:, 2 * h + jx, u : 256 : 2], ident[:])
+                    nc.tensor.transpose(gt[:, o : o + P], gw[:, jx, u : 256 : 2], ident[:])
 
         def gview(k):
-            i, h = divmod(k, 2)
-            a, g, tg = CHUNKS[i]
-            c0 = 512 * tg + 256 * h
-            gv = gts[k][:].bitcast(BF16).rearrange("p (u k e) -> p u k e", u=2, e=2)
-            return gv, tab[:, 2 * g : 2 * g + 2, :, c0 : c0 + 256]
+            a, g, r = CELLS[k]
+            c0 = 256 * r
+            gv = gts[k][:].bitcast(BF16).rearrange("p (u k e) -> p k u e", u=2, e=2)
+            return gv, tab[:, 2 * g : 2 * g + 2, :, c0 : c0 + 256].rearrange("p u c k -> p c k u")
 
         def prod_cos(k):
             gv, tb = gview(k)
-            pp = prod.tile([P, 2, 512], F32, tag="pp", name="pp", align_bytes=64)
+            pp = prod.tile([P, 1024], F32, tag="pp", name="pp", align_bytes=64)
             qq = prod.tile([P, 2, 512], F32, tag="qq", name="qq", align_bytes=64)
             pqs[k] = pp, qq
-            cb = tb[:, :, 0, :].unsqueeze(3).to_broadcast([P, 2, 256, 2])
-            nc.vector.tensor_tensor(out=pp[:].rearrange("p u (k e) -> p u k e", e=2), in0=gv, in1=cb, op=ALU.mult)
+            cb = tb[:, 0].unsqueeze(3).to_broadcast([P, 256, 2, 2])
+            nc.vector.tensor_tensor(out=pp[:].rearrange("p (k u e) -> p k u e", u=2, e=2), in0=gv, in1=cb, op=ALU.mult)
 
-        def prod_sin(k, e, u=None):
+        def prod_sin(k, e, lo=0, hi=256):
             gv, tb = gview(k)
-            us = slice(0, 2) if u is None else slice(u, u + 1)
             nc.vector.scalar_tensor_tensor(
-                out=pqs[k][1][:, e, :].rearrange("p (u k) -> p u k", u=2)[:, us], in0=gv[:, us, :, 1 - e],
-                scalar=1.0 - 2.0 * e, in1=tb[:, us, 1, :], op0=ALU.mult, op1=ALU.mult)
+                out=pqs[k][1][:, e, 2 * lo : 2 * hi].rearrange("p (k u) -> p k u", u=2), in0=gv[:, lo:hi, :, 1 - e],
+                scalar=1.0 - 2.0 * e, in1=tb[:, 1, lo:hi], op0=ALU.mult, op1=ALU.mult)
 
         def add(k, engine, lo, hi):
-            i, h = divmod(k, 2)
+            a, g, r = CELLS[k]
+            i, h = (a, g, r // 2), r % 2
             if i not in dfeat:
-                d = dpool.tile([P, 2048], BF16, tag="dfeat", name="dfeat", align_bytes=64)
+                d = dpool.tile([P, 2048], BF16, tag="dfeat", name="dfeat", align_bytes=64, bufs=DFEAT)
                 dfeat[i] = d
             pp, qq = pqs[k]
             o = 1024 * h
             engine.tensor_tensor(
-                out=dfeat[i][:, o + 4 * lo : o + 4 * hi].rearrange("p (k u e) -> p k u e", u=2, e=2),
-                in0=pp[:].rearrange("p u (k e) -> p k u e", e=2)[:, lo:hi],
-                in1=qq[:].rearrange("p e (u k) -> p k u e", u=2)[:, lo:hi], op=ALU.add)
+                out=dfeat[i][:, o + 4 * lo : o + 4 * hi].rearrange("p (n e) -> p n e", e=2),
+                in0=pp[:, 4 * lo : 4 * hi].rearrange("p (n e) -> p n e", e=2),
+                in1=qq[:, :, 2 * lo : 2 * hi].rearrange("p e n -> p n e"), op=ALU.add)
 
-        def quant_feat(i, lo=0, hi=2):
-            a, g, tg = CHUNKS[i]
-            cols = slice(512 * tg + 256 * lo, 512 * tg + 256 * hi)
-            nc.vector.quantize_mx(out=fc[a, g][:, cols].bitcast(E5M2), scales=fs[a, g][:, cols], in_=dfeat[i][:, 1024 * lo : 1024 * hi])
+        def quant_feat(k):
+            a, g, r = CELLS[k]
+            cols = slice(256 * r, 256 * r + 256)
+            o = 1024 * (r % 2)
+            nc.vector.quantize_mx(out=fc[a, g][:, cols].bitcast(E5M2), scales=fs[a, g][:, cols], in_=dfeat[a, g, r // 2][:, o : o + 1024])
 
         def d_turn(i, u, eng="S"):
             if i not in dtok:
@@ -219,9 +233,9 @@ def tile_multiscaleretention_pa_v_kernel(tc, x, w_q, w_k, grad_0, grad_1, out_0,
             cp(out=dv, in_=dt[:].bitcast(BF16).rearrange("q (j p e) -> q p e j", j=4, e=2))
 
         def quant_tok(i):
-            a, g, tg = CHUNKS[i]
-            cols = slice(512 * g, 512 * (g + 1))
-            nc.vector.quantize_mx(out=kc[a][:, tg, cols].bitcast(E5M2), scales=ks[a][:, tg, cols], in_=dtok[i][:])
+            a, g, tg = i
+            codes, scales = tok_codes((a, g))
+            nc.vector.quantize_mx(out=codes[:, tg].bitcast(E5M2), scales=scales[:, tg], in_=dtok[i][:])
 
         wide = {}
 
@@ -264,10 +278,11 @@ def tile_multiscaleretention_pa_v_kernel(tc, x, w_q, w_k, grad_0, grad_1, out_0,
             acc = psum.tile([P, 512], F32, tag="acc", name="acc", bufs=4)
             m = slice(P * eb, P * (eb + 1))
             n = slice(512 * g, 512 * (g + 1))
+            codes, scales = tok_codes((a, g))
             for tg in range(2):
                 nc.tensor.matmul_mx(
                     out=acc[:], lhsT=xc[:, tg, m].bitcast(E4M3), lhsT_scale=xs[:, tg, m],
-                    rhs=kc[a][:, tg, n].bitcast(E5M2), rhs_scale=ks[a][:, tg, n], start=(tg == 0), stop=(tg == 1))
+                    rhs=codes[:, tg].bitcast(E5M2), rhs_scale=scales[:, tg], start=(tg == 0), stop=(tg == 1))
             return acc, dw_hbm[a][m, n]
 
         def dx_mm(tg, j, h):
@@ -280,97 +295,107 @@ def tile_multiscaleretention_pa_v_kernel(tc, x, w_q, w_k, grad_0, grad_1, out_0,
                     rhs=wc[a, g][:, n].bitcast(E4M3), rhs_scale=ws[a, g][:, n], start=(s == 0), stop=(s == 3))
             return acc, dx_hbm[:, tg, j, n]
 
-        ctx.enter_context(tc.manual_schedule())
         V, G = nc.vector, nc.gpsimd
-        at = CHUNKS.index
-        for what in LOADS:
-            (load_g if what[0] == "g" else load_x if what[0] == "x" else load_w)(*what[1:])
-        seeds_phase(0)
-        seeds_phase(1)
-        seeds_sin(0)
-        g_turn(0)
-        for k in range(2):
-            for u in range(2):
-                level_s(u, k)
-                level_v(u, k)
-        seeds_sin(1)
+        NC = len(CELLS)
+        at = CELLS.index
         w_units = [(a, h, g) for h in range(2) for a in range(2) for g in range(2)]
         x_units = [(tg, h) for tg in range(2) for h in range(2)]
-        L = {k: [] for k in range(-1, 17)}
-        S_ = {k: [] for k in range(-1, 17)}
+        L = {k: [] for k in range(-1, NC + 2)}
+        S_ = {k: [] for k in range(-1, NC + 2)}
         for gu, k, when in TABLE:
-            S_[when - 1].append((gu, k))
-            L[when].append(lambda gu=gu, k=k: level_v(gu, k))
-        for gu, k in S_[-1]:
-            level_s(gu, k)
+            if when >= 0:
+                S_[when - 1].append((gu, k))
+                L[when].append(lambda gu=gu, k=k: level_v(gu, k))
         for n, u in enumerate(x_units):
             L[XS + n + 1].append(lambda u=u: x_quant(*u))
+        WAT = [WS + n for n in range(8)] if isinstance(WS, int) else WS
         for n, u in enumerate(w_units):
-            L[WS + n + 1].append(lambda u=u: w_quant(*u))
+            L[WAT[n] + 1].append(lambda u=u: w_quant(*u))
+        turns, toks = {}, {}
         mx = []
         for a in range(2):
             for g in range(2):
-                i = max(at((a, g, tg)) for tg in range(2))
-                mx.append((2 * i + 4 - FAST, 0, [lambda a=a, g=g, e=e: dw_mm(a, g, e) for e in range(8)]))
-        for tg in range(2):
-            i = max(at((a, g, tg)) for a in range(2) for g in range(2))
-            mx.append((2 * i + 3, 1, [lambda tg=tg, j=j, h=h: dx_mm(tg, j, h) for j in range(4) for h in range(2)]))
+                last = 0
+                for tg in range(2):
+                    kl = max(at((a, g, 2 * tg + h)) for h in range(2))
+                    last = max(last, kl)
+                    turns.setdefault(kl + 1, []).append((a, g, tg))
+                    toks.setdefault(kl + 2, []).append((a, g, tg))
+                mx.append((max(last + 3, XS + 6), 0, [(2, lambda a=a, g=g, e=e: dw_mm(a, g, e)) for e in range(8)]))
+        for r in range(4):
+            kr = max(at((a, g, r)) for a in range(2) for g in range(2))
+            for h in range(2):
+                ready = max(WAT[4 * h : 4 * h + 4]) + 2
+                mx.append((max(kr + 2, ready), 1, [(4, lambda r=r, j=j, h=h: dx_mm(r // 2, 2 * (r % 2) + j, h)) for j in range(2)]))
         mx.sort(key=lambda m: (m[0], m[1]))
-        mx = [(av, 4 if kind else 2, f) for av, kind, fs_ in mx for f in fs_]
-        cnt = 0
-        for k in range(16):
-            i = k // 2
-            if k + 1 < 16:
-                g_turn(k + 1)
+        mx = [(av, n, f) for av, kind, fs_ in mx for n, f in fs_]
+        pend = []
+
+        def groups(k, limit):
             n = 0
-            exits = []
-            while mx and mx[0][0] <= k and n + mx[0][1] <= MXHALF:
+            while mx and mx[0][0] <= k and n + mx[0][1] <= limit:
                 n += mx[0][1]
-                if len(exits) == 3:
-                    leave(*exits.pop(0), "S")
-                exits.append(mx.pop(0)[2]())
-            for acc, dst in exits:
-                leave(acc, dst, "S")
-            if k % 2 == 0 and i >= 1 and FAST:
-                d_turn(i - 1, 0)
+                if len(pend) == 3:
+                    leave(*pend.pop(0), "S")
+                pend.append(mx.pop(0)[2]())
+            while pend:
+                leave(*pend.pop(0), "S")
+
+        g_turn(0)
+        for gu, k, when in TABLE:
+            if when < 0:
+                level_s(gu, k)
+                level_v(gu, k)
+        for gu, k in S_[-1]:
+            level_s(gu, k)
+        for k in range(NC):
+            if k + 1 < NC:
+                g_turn(k + 1)
+            groups(k, MXA)
             prod_cos(k)
             prod_sin(k, 0)
             if k >= 1 and GTOK < 256 and k - 1 not in VK:
                 add(k - 1, V, GTOK, 256)
-            if k % 2 == 0 and i >= 1:
-                quant_feat(i - 1)
-                if not FAST:
-                    d_turn(i - 1, 0)
-                d_turn(i - 1, 1)
-            if WS <= k < WS + 8:
-                a, h, g = w_units[k - WS]
+            if k >= 1:
+                quant_feat(k - 1)
+            for c in turns.get(k, []):
+                d_turn(c, 0)
+                d_turn(c, 1)
+            groups(k, MXB)
+            if k in WAT:
+                a, h, g = w_units[WAT.index(k)]
                 w_turn(a, h, g, 0, "S")
                 w_turn(a, h, g, 1, "S")
-            if k % 2 == 1 and i >= 1:
-                quant_tok(i - 1)
+            for c in toks.get(k, []):
+                quant_tok(c)
             if XS <= k < XS + 4:
-                tg, h = x_units[k - XS]
-                x_lay(tg, h, "S")
+                x_lay(*x_units[k - XS], "S")
             for f in L[k]:
                 f()
             for gu, kk in S_[k]:
                 level_s(gu, kk)
-            if k == 15:
-                quant_feat(7, 0, 1)
-            prod_sin(k, 1, 0)
-            prod_sin(k, 1, 1)
+            prod_sin(k, 1, 0, QCUT)
+            if QCUT < 256:
+                prod_sin(k, 1, QCUT, 256)
             if k in VK:
                 add(k, V, 0, 256)
             elif GTOK > 0:
                 add(k, G, 0, GTOK)
-        d_turn(7, 0, "S")
-        d_turn(7, 1, "V")
-        quant_feat(7, 1, 2)
-        last = [m for m in mx if m[0] > 17]
-        mx = [m for m in mx if m[0] <= 17]
+        if NC - 1 not in VK:
+            add(NC - 1, V, GTOK, 256)
+        quant_feat(NC - 1)
+        for c in turns[NC]:
+            d_turn(c, 0, "S")
+            d_turn(c, 1, "V")
+        cnt = 0
+        last = [m for m in mx if m[0] > NC + 1]
+        mx = [m for m in mx if m[0] <= NC + 1]
+        for c in toks.get(NC, []):
+            quant_tok(c)
         while mx or last:
             acc, dst = (mx or last).pop(0)[2]()
             leave(acc, dst, "SV"[cnt % 2])
             cnt += 1
             if cnt == 4:
-                quant_tok(7)
+                for c in toks[NC + 1]:
+                    quant_tok(c)

@@ -21,19 +21,22 @@ N = P + 3
 
 FLOPS = 2 * 2 * T * E * 2 * C
 
-CELLS = [(0, 0, 0), (0, 1, 0), (1, 0, 0), (1, 1, 0), (0, 0, 1), (0, 0, 2), (0, 0, 3), (0, 1, 1), (1, 0, 1), (1, 1, 1), (0, 1, 2), (0, 1, 3), (1, 0, 2), (1, 1, 2), (1, 0, 3), (1, 1, 3)]
+CELLS = [(0, 0, 0), (1, 0, 0), (0, 1, 0), (1, 1, 0), (0, 0, 1), (0, 0, 2), (0, 0, 3), (0, 1, 1), (1, 0, 1), (1, 1, 1), (0, 1, 2), (0, 1, 3), (1, 0, 2), (1, 1, 2), (1, 0, 3), (1, 1, 3)]
 STAGE = 8
 MXA = 4
 MXB = 8
 LEVELS = [(0, 128, 128), (0, 256, 256), (0, 512, 512)]
-GBUFS = 6
-DFEAT = 6
-QCUT = 256
-LOADS = [("g", 0, 0, 0), ("w",0,0), ("g", 0, 1, 0), ("w",1,0), ("g", 1, 0, 0), ("g", 1, 1, 0), ("x",0), ("g", 0, 0, 1), ("w",0,1), ("g", 0, 0, 2), ("g", 0, 0, 3), ("x",1), ("g", 0, 1, 1), ("g", 1, 0, 1), ("w",1,1), ("g", 1, 1, 1), ("g", 0, 1, 2), ("g", 0, 1, 3), ("g", 1, 0, 2), ("g", 1, 1, 2), ("g", 1, 0, 3), ("g", 1, 1, 3)]
-TABLE = [(0,0,-1),(1,0,-1),(2,0,0),(3,0,0),(0,1,1),(1,1,1),(0,2,3),(1,2,4),(2,1,5),(3,1,5),(2,2,7),(3,2,8)]
-WS = [0, 1, 2, 3, 6, 7, 8, 9]
+GBUFS = 5
+DFEAT = 5
+QCUT = 224
+KC = 3
+XB = 1
+WB = 2
+LOADS = [("g", 0, 0, 0), ("w",0,0), ("g", 1, 0, 0), ("w",1,0), ("g", 0, 1, 0), ("g", 1, 1, 0), ("w",0,1), ("g", 0, 0, 1), ("x",0), ("w",1,1), ("g", 0, 0, 2), ("g", 0, 0, 3), ("x",1), ("g", 0, 1, 1), ("g", 1, 0, 1), ("g", 1, 1, 1), ("g", 0, 1, 2), ("g", 0, 1, 3), ("g", 1, 0, 2), ("g", 1, 1, 2), ("g", 1, 0, 3), ("g", 1, 1, 3)]
+TABLE = [(0,0,-1),(1,0,-1),(2,0,0),(3,0,0),(0,1,1),(1,1,1),(0,2,2),(1,2,3),(2,1,4),(3,1,4),(2,2,5),(3,2,6)]
+WS = [0, 0, 1, 1, 2, 2, 3, 3]
 XS = 3
-GTOK = 0
+GTOK = 160
 VK = (15,)
 
 
@@ -60,17 +63,17 @@ def tile_multiscaleretention_pa_v_kernel(tc, x, w_q, w_k, grad_0, grad_1, out_0,
             graw[a, g, r] = t
 
         def load_x(tg):
-            t = raw.tile([P, 4, E], BF16, tag="xraw", name="xraw", align_bytes=64, bufs=2)
+            t = raw.tile([P, 4, E], BF16, tag="xraw", name="xraw", align_bytes=64, bufs=XB)
             nc.sync.dma_start(out=t[:], in_=x_hbm[:, tg])
             xraw[tg] = t
 
         def load_w(a, h):
-            t = raw.tile([P, 4, C], BF16, tag="wraw", name="wraw", align_bytes=64, bufs=3)
+            t = raw.tile([P, 4, C], BF16, tag="wraw", name="wraw", align_bytes=64, bufs=WB)
             nc.sync.dma_start(out=t[:], in_=w_hbm[a][:, h])
             wraw[a, h] = t
 
 
-        tab = keep.tile([P, 4, 2, T], F32)
+        tab = keep.tile([P, 4, 3, T], F32)
         zk = keep.tile([P, 4, 3, 3], F32)
         with tc.tile_pool(name="seed", bufs=1) as seed:
             tt = seed.tile([P, N], F32)
@@ -125,6 +128,7 @@ def tile_multiscaleretention_pa_v_kernel(tc, x, w_q, w_k, grad_0, grad_1, out_0,
                 for k, f in ((0, cs), (1, sn)):
                     nc.vector.tensor_tensor(out=tab[:, gs, k, 0:P], in0=f[:, :, 0:P], in1=rr[:, gs, 0:P], op=ALU.mult)
                 nc.vector.tensor_scalar(out=zk[:, gs, 2, :], in0=zk[:, gs, 1, :], scalar1=-1.0, scalar2=None, op0=ALU.mult)
+                nc.vector.tensor_scalar(out=tab[:, gs, 2, 0:P], in0=tab[:, gs, 1, 0:P], scalar1=-1.0, scalar2=None, op0=ALU.mult)
 
             for what in LOADS:
                 (load_g if what[0] == "g" else load_x if what[0] == "x" else load_w)(*what[1:])
@@ -149,8 +153,12 @@ def tile_multiscaleretention_pa_v_kernel(tc, x, w_q, w_k, grad_0, grad_1, out_0,
         def level_v(gu, k):
             src, dst, n = LEVELS[k]
             nc.vector.scalar_tensor_tensor(
-                out=tab[:, gu, :, dst : dst + n], in0=tab[:, gu, :, src : src + n], scalar=zk[:, gu, 0, k : k + 1],
+                out=tab[:, gu, 0:2, dst : dst + n], in0=tab[:, gu, 0:2, src : src + n], scalar=zk[:, gu, 0, k : k + 1],
                 in1=tmps[gu, k][:, :, 0:n], op0=ALU.mult, op1=ALU.add)
+
+        def level_n(gu, k):
+            src, dst, n = LEVELS[k]
+            nc.scalar.activation(out=tab[:, gu, 2, dst : dst + n], in_=tab[:, gu, 1, dst : dst + n], func=ACT.Copy, scale=-1.0)
 
         xc = keep.tile([P, 2, E], U32, align_bytes=64)
         xs = keep.tile([P, 2, E], U8, align_bytes=64)
@@ -165,7 +173,7 @@ def tile_multiscaleretention_pa_v_kernel(tc, x, w_q, w_k, grad_0, grad_1, out_0,
         def tok_codes(f):
             if f not in kc:
                 for d, nm, dt in ((kc, "kc", U32), (ks, "ks", U8)):
-                    t = dpool.tile([P, 2, 512], dt, tag=nm, name=nm, align_bytes=64, bufs=3)
+                    t = dpool.tile([P, 2, 512], dt, tag=nm, name=nm, align_bytes=64, bufs=KC)
                     d[f] = t
             return kc[f], ks[f]
 
@@ -190,16 +198,16 @@ def tile_multiscaleretention_pa_v_kernel(tc, x, w_q, w_k, grad_0, grad_1, out_0,
         def prod_cos(k):
             gv, tb = gview(k)
             pp = prod.tile([P, 1024], F32, tag="pp", name="pp", align_bytes=64)
-            qq = prod.tile([P, 2, 512], F32, tag="qq", name="qq", align_bytes=64)
+            qq = prod.tile([P, 1024], F32, tag="qq", name="qq", align_bytes=64)
             pqs[k] = pp, qq
             cb = tb[:, 0].unsqueeze(3).to_broadcast([P, 256, 2, 2])
             nc.vector.tensor_tensor(out=pp[:].rearrange("p (k u e) -> p k u e", u=2, e=2), in0=gv, in1=cb, op=ALU.mult)
 
-        def prod_sin(k, e, lo=0, hi=256):
+        def prod_sin(k, lo, hi):
             gv, tb = gview(k)
-            nc.vector.scalar_tensor_tensor(
-                out=pqs[k][1][:, e, 2 * lo : 2 * hi].rearrange("p (k u) -> p k u", u=2), in0=gv[:, lo:hi, :, 1 - e],
-                scalar=1.0 - 2.0 * e, in1=tb[:, 1, lo:hi], op0=ALU.mult, op1=ALU.mult)
+            nc.vector.tensor_tensor(
+                out=pqs[k][1][:, 4 * lo : 4 * hi].rearrange("p (k u e) -> p k u e", u=2, e=2), in0=gv[:, lo:hi, :, ::-1],
+                in1=tb[:, 1:3, lo:hi].rearrange("p e k u -> p k u e"), op=ALU.mult)
 
         def add(k, engine, lo, hi):
             a, g, r = CELLS[k]
@@ -209,10 +217,7 @@ def tile_multiscaleretention_pa_v_kernel(tc, x, w_q, w_k, grad_0, grad_1, out_0,
                 dfeat[i] = d
             pp, qq = pqs[k]
             o = 1024 * h
-            engine.tensor_tensor(
-                out=dfeat[i][:, o + 4 * lo : o + 4 * hi].rearrange("p (n e) -> p n e", e=2),
-                in0=pp[:, 4 * lo : 4 * hi].rearrange("p (n e) -> p n e", e=2),
-                in1=qq[:, :, 2 * lo : 2 * hi].rearrange("p e n -> p n e"), op=ALU.add)
+            engine.tensor_tensor(out=dfeat[i][:, o + 4 * lo : o + 4 * hi], in0=pp[:, 4 * lo : 4 * hi], in1=qq[:, 4 * lo : 4 * hi], op=ALU.add)
 
         def quant_feat(k):
             a, g, r = CELLS[k]
@@ -311,6 +316,10 @@ def tile_multiscaleretention_pa_v_kernel(tc, x, w_q, w_k, grad_0, grad_1, out_0,
         WAT = [WS + n for n in range(8)] if isinstance(WS, int) else WS
         for n, u in enumerate(w_units):
             L[WAT[n] + 1].append(lambda u=u: w_quant(*u))
+        N_ = {k: [] for k in range(-1, NC + 2)}
+        for gu, k, when in TABLE:
+            if when >= 0:
+                N_[when + 1].append((gu, k))
         turns, toks = {}, {}
         mx = []
         for a in range(2):
@@ -321,7 +330,7 @@ def tile_multiscaleretention_pa_v_kernel(tc, x, w_q, w_k, grad_0, grad_1, out_0,
                     last = max(last, kl)
                     turns.setdefault(kl + 1, []).append((a, g, tg))
                     toks.setdefault(kl + 2, []).append((a, g, tg))
-                mx.append((max(last + 3, XS + 6), 0, [(2, lambda a=a, g=g, e=e: dw_mm(a, g, e)) for e in range(8)]))
+                mx.append((max(last + 2, XS + 6), 0, [(2, lambda a=a, g=g, e=e: dw_mm(a, g, e)) for e in range(8)]))
         for r in range(4):
             kr = max(at((a, g, r)) for a in range(2) for g in range(2))
             for h in range(2):
@@ -346,43 +355,46 @@ def tile_multiscaleretention_pa_v_kernel(tc, x, w_q, w_k, grad_0, grad_1, out_0,
             if when < 0:
                 level_s(gu, k)
                 level_v(gu, k)
+                level_n(gu, k)
         for gu, k in S_[-1]:
             level_s(gu, k)
         for k in range(NC):
             if k + 1 < NC:
                 g_turn(k + 1)
-            groups(k, MXA)
+            for gu, kk in N_[k]:
+                level_n(gu, kk)
+            groups(k - 1, MXA)
             prod_cos(k)
-            prod_sin(k, 0)
+            prod_sin(k, 0, QCUT)
+            for c in toks.get(k, []):
+                quant_tok(c)
             if k >= 1 and GTOK < 256 and k - 1 not in VK:
-                add(k - 1, V, GTOK, 256)
+                add(k - 1, V, 0, 256 - GTOK)
             if k >= 1:
                 quant_feat(k - 1)
             for c in turns.get(k, []):
                 d_turn(c, 0)
                 d_turn(c, 1)
             groups(k, MXB)
-            if k in WAT:
-                a, h, g = w_units[WAT.index(k)]
-                w_turn(a, h, g, 0, "S")
-                w_turn(a, h, g, 1, "S")
-            for c in toks.get(k, []):
-                quant_tok(c)
+            for n in range(8):
+                if WAT[n] == k:
+                    a, h, g = w_units[n]
+                    w_turn(a, h, g, 0, "S")
+                    w_turn(a, h, g, 1, "S")
             if XS <= k < XS + 4:
                 x_lay(*x_units[k - XS], "S")
             for f in L[k]:
                 f()
             for gu, kk in S_[k]:
                 level_s(gu, kk)
-            prod_sin(k, 1, 0, QCUT)
             if QCUT < 256:
-                prod_sin(k, 1, QCUT, 256)
+                prod_sin(k, QCUT, 256)
             if k in VK:
                 add(k, V, 0, 256)
             elif GTOK > 0:
-                add(k, G, 0, GTOK)
+                add(k, G, 256 - GTOK, 256)
         if NC - 1 not in VK:
-            add(NC - 1, V, GTOK, 256)
+            add(NC - 1, V, 0, 256 - GTOK)
         quant_feat(NC - 1)
         for c in turns[NC]:
             d_turn(c, 0, "S")

@@ -22,7 +22,7 @@ N = P + 3
 FLOPS = 2 * 2 * T * E * 2 * C
 
 CELLS = [(0, 0, 0), (1, 0, 0), (0, 1, 0), (1, 1, 0), (0, 0, 1), (0, 0, 2), (0, 0, 3), (0, 1, 1), (1, 0, 1), (1, 1, 1), (0, 1, 2), (0, 1, 3), (1, 0, 2), (1, 1, 2), (1, 0, 3), (1, 1, 3)]
-STAGE = 8
+STAGE = 12
 MXA = 4
 MXB = 8
 LEVELS = [(0, 128, 128), (0, 256, 256), (0, 512, 512)]
@@ -38,6 +38,9 @@ WS = [0, 0, 1, 1, 2, 2, 3, 3]
 XS = 3
 GTOK = 160
 VK = (15,)
+EARLY = 1
+SFIRST = 0
+TMP = 2
 
 
 def tile_multiscaleretention_pa_v_kernel(tc, x, w_q, w_k, grad_0, grad_1, out_0, out_1, out_2):
@@ -53,7 +56,6 @@ def tile_multiscaleretention_pa_v_kernel(tc, x, w_q, w_k, grad_0, grad_1, out_0,
         psum = ctx.enter_context(tc.psum_pool(name="psum", bufs=2))
         raw = ctx.enter_context(tc.tile_pool(name="raw", bufs=3))
 
-        ctx.enter_context(tc.manual_schedule())
         graw, xraw, wraw = {}, {}, {}
 
         def load_g(a, g, r):
@@ -83,9 +85,9 @@ def tile_multiscaleretention_pa_v_kernel(tc, x, w_q, w_k, grad_0, grad_1, out_0,
             nc.vector.memset(tenk[:], 10000.0)
             ex = seed.tile([P, 4], F32)
             nc.gpsimd.tensor_scalar(out=ex[:], in0=jj[:], scalar1=-2.0 / C, scalar2=0.0, op0=ALU.mult, op1=ALU.add)
+            nc.gpsimd.iota(tt[:, 0:P], pattern=[[4, P]], base=0, channel_multiplier=0, allow_small_or_imprecise_dtypes=True)
             ww = seed.tile([P, 4], F32)
             nc.gpsimd.tensor_tensor(out=ww[:], in0=tenk[:], in1=ex[:], op=ALU.pow)
-            nc.gpsimd.iota(tt[:, 0:P], pattern=[[4, P]], base=0, channel_multiplier=0, allow_small_or_imprecise_dtypes=True)
             for k, v in enumerate((1.0, 2.0, 512.0)):
                 nc.vector.memset(tt[:, P + k : P + k + 1], v)
             ident = keep.tile([P, P], F32)
@@ -145,7 +147,7 @@ def tile_multiscaleretention_pa_v_kernel(tc, x, w_q, w_k, grad_0, grad_1, out_0,
 
         def level_s(gu, k):
             src, dst, n = LEVELS[k]
-            tmp = prod.tile([P, 2, 512], F32, tag="tmp", name="tmp", align_bytes=64)
+            tmp = prod.tile([P, 2, 512], F32, tag="tmp", name="tmp", align_bytes=64, bufs=TMP)
             tmps[gu, k] = tmp
             for b in range(2):
                 nc.scalar.activation(out=tmp[:, b, 0:n], in_=tab[:, gu, 1 - b, src : src + n], func=ACT.Copy, scale=zk[:, gu, 2 - b, k : k + 1])
@@ -201,13 +203,13 @@ def tile_multiscaleretention_pa_v_kernel(tc, x, w_q, w_k, grad_0, grad_1, out_0,
             qq = prod.tile([P, 1024], F32, tag="qq", name="qq", align_bytes=64)
             pqs[k] = pp, qq
             cb = tb[:, 0].unsqueeze(3).to_broadcast([P, 256, 2, 2])
-            nc.vector.tensor_tensor(out=pp[:].rearrange("p (k u e) -> p k u e", u=2, e=2), in0=gv, in1=cb, op=ALU.mult)
+            nc.vector.tensor_tensor(out=pp[:].rearrange("p (k u e) -> p k u e", u=2, e=2), in0=cb, in1=gv, op=ALU.mult)
 
         def prod_sin(k, lo, hi):
             gv, tb = gview(k)
             nc.vector.tensor_tensor(
-                out=pqs[k][1][:, 4 * lo : 4 * hi].rearrange("p (k u e) -> p k u e", u=2, e=2), in0=gv[:, lo:hi, :, ::-1],
-                in1=tb[:, 1:3, lo:hi].rearrange("p e k u -> p k u e"), op=ALU.mult)
+                out=pqs[k][1][:, 4 * lo : 4 * hi].rearrange("p (k u e) -> p k u e", u=2, e=2), in0=tb[:, 1:3, lo:hi].rearrange("p e k u -> p k u e"),
+                in1=gv[:, lo:hi, :, ::-1], op=ALU.mult)
 
         def add(k, engine, lo, hi):
             a, g, r = CELLS[k]
@@ -363,13 +365,19 @@ def tile_multiscaleretention_pa_v_kernel(tc, x, w_q, w_k, grad_0, grad_1, out_0,
                 g_turn(k + 1)
             for gu, kk in N_[k]:
                 level_n(gu, kk)
+            if SFIRST:
+                for gu, kk in S_[k]:
+                    level_s(gu, kk)
             groups(k - 1, MXA)
             prod_cos(k)
             prod_sin(k, 0, QCUT)
-            for c in toks.get(k, []):
-                quant_tok(c)
             if k >= 1 and GTOK < 256 and k - 1 not in VK:
                 add(k - 1, V, 0, 256 - GTOK)
+            for c in toks.get(k, []):
+                quant_tok(c)
+            early = L[k][: (1 if EARLY else 0)] if not toks.get(k) else []
+            for f in early:
+                f()
             if k >= 1:
                 quant_feat(k - 1)
             for c in turns.get(k, []):
@@ -383,10 +391,11 @@ def tile_multiscaleretention_pa_v_kernel(tc, x, w_q, w_k, grad_0, grad_1, out_0,
                     w_turn(a, h, g, 1, "S")
             if XS <= k < XS + 4:
                 x_lay(*x_units[k - XS], "S")
-            for f in L[k]:
+            for f in L[k][len(early) :]:
                 f()
-            for gu, kk in S_[k]:
-                level_s(gu, kk)
+            if not SFIRST:
+                for gu, kk in S_[k]:
+                    level_s(gu, kk)
             if QCUT < 256:
                 prod_sin(k, QCUT, 256)
             if k in VK:

import math
from contextlib import ExitStack

import concourse.mybir as mybir
from concourse.masks import make_identity

F32 = mybir.dt.float32
BF16 = mybir.dt.bfloat16
U32 = mybir.dt.uint32
I32 = mybir.dt.int32
U8 = mybir.dt.uint8
E4M3 = mybir.dt.float8_e4m3fn_x4
E5M2 = mybir.dt.float8_e5m2_x4
ALU = mybir.AluOpType
ACT = mybir.ActivationFunctionType

P = 128
T, E, C = 1024, 1024, 1024
XPOS_BASE = 512.0
N = P + 3

FLOPS = 2 * 2 * T * E * 2 * C

CELLS = [(0, 0, 0), (1, 0, 0), (0, 1, 0), (1, 1, 0), (0, 0, 1), (0, 0, 2), (0, 0, 3), (0, 1, 1), (1, 0, 1), (1, 1, 1), (0, 1, 2), (0, 1, 3), (1, 0, 2), (1, 1, 2), (1, 0, 3), (1, 1, 3)]
STAGE = 12
MXA = 4
MXB = 8
LEVELS = [(0, 128, 128), (0, 256, 256), (0, 512, 512)]
GBUFS = 5
DFEAT = 5
QCUT = 224
KC = 3
XB = 1
WB = 2
LOADS = [("g", 0, 0, 0), ("w",0,0), ("g", 1, 0, 0), ("w",1,0), ("g", 0, 1, 0), ("g", 1, 1, 0), ("w",0,1), ("g", 0, 0, 1), ("x",0), ("w",1,1), ("g", 0, 0, 2), ("g", 0, 0, 3), ("x",1), ("g", 0, 1, 1), ("g", 1, 0, 1), ("g", 1, 1, 1), ("g", 0, 1, 2), ("g", 0, 1, 3), ("g", 1, 0, 2), ("g", 1, 1, 2), ("g", 1, 0, 3), ("g", 1, 1, 3)]
TABLE = [(0,0,-1),(1,0,-1),(2,0,0),(3,0,0),(0,1,1),(1,1,1),(0,2,2),(1,2,3),(2,1,4),(3,1,4),(2,2,5),(3,2,6)]
WS = [0, 0, 1, 1, 2, 2, 3, 3]
XS = 3
GTOK = 160
VK = (15,)
EARLY = 1
SFIRST = 0
TMP = 2


def tile_multiscaleretention_pa_v_kernel(tc, x, w_q, w_k, grad_0, grad_1, out_0, out_1, out_2):
    nc = tc.nc
    x_hbm = x[0].rearrange("(g p j) e -> p g j e", g=2, j=4)
    g_hbm = [g[0].rearrange("(g p j) e -> p g j e", g=2, j=4) for g in (grad_0, grad_1)]
    w_hbm = [w.rearrange("(h t p) c -> p h t c", h=2, t=4) for w in (w_q, w_k)]
    dx_hbm = out_0[0].rearrange("(g p j) e -> p g j e", g=2, j=4)
    dw_hbm = [out_1, out_2]

    with ExitStack() as ctx:
        keep = ctx.enter_context(tc.tile_pool(name="keep", bufs=1))
        psum = ctx.enter_context(tc.psum_pool(name="psum", bufs=2))
        raw = ctx.enter_context(tc.tile_pool(name="raw", bufs=3))

        graw, xraw, wraw = {}, {}, {}

        def load_g(a, g, r):
            tg, h = divmod(r, 2)
            t = raw.tile([P, 2, 512], BF16, tag="graw", name="graw", align_bytes=64, bufs=GBUFS)
            nc.sync.dma_start(out=t[:], in_=g_hbm[a][:, tg, 2 * h : 2 * h + 2, 512 * g : 512 * (g + 1)])
            graw[a, g, r] = t

        def load_x(tg):
            t = raw.tile([P, 4, E], BF16, tag="xraw", name="xraw", align_bytes=64, bufs=XB)
            nc.sync.dma_start(out=t[:], in_=x_hbm[:, tg])
            xraw[tg] = t

        def load_w(a, h):
            t = raw.tile([P, 4, C], BF16, tag="wraw", name="wraw", align_bytes=64, bufs=WB)
            nc.sync.dma_start(out=t[:], in_=w_hbm[a][:, h])
            wraw[a, h] = t


        tab = keep.tile([P, 4, 3, T], F32)
        zk = keep.tile([P, 4, 3, 3], F32)
        with tc.tile_pool(name="seed", bufs=1) as seed:
            tt = seed.tile([P, N], F32)
            jj = seed.tile([P, 4], F32)
            nc.gpsimd.iota(jj[:].rearrange("p (g u) -> p g u", u=2), pattern=[[256, 2], [1, 2]], base=0, channel_multiplier=2, allow_small_or_imprecise_dtypes=True)
            tenk = seed.tile([P, 4], F32)
            nc.vector.memset(tenk[:], 10000.0)
            ex = seed.tile([P, 4], F32)
            nc.gpsimd.tensor_scalar(out=ex[:], in0=jj[:], scalar1=-2.0 / C, scalar2=0.0, op0=ALU.mult, op1=ALU.add)
            nc.gpsimd.iota(tt[:, 0:P], pattern=[[4, P]], base=0, channel_multiplier=0, allow_small_or_imprecise_dtypes=True)
            ww = seed.tile([P, 4], F32)
            nc.gpsimd.tensor_tensor(out=ww[:], in0=tenk[:], in1=ex[:], op=ALU.pow)
            for k, v in enumerate((1.0, 2.0, 512.0)):
                nc.vector.memset(tt[:, P + k : P + k + 1], v)
            ident = keep.tile([P, P], F32)
            make_identity(nc, ident[:])
            dd = seed.tile([P, 4], F32)
            nc.vector.tensor_scalar(out=dd[:], in0=jj[:], scalar1=2.0 / (1.4 * C), scalar2=0.4 / 1.4, op0=ALU.mult, op1=ALU.add)
            lnd = seed.tile([P, 4], F32)
            nc.scalar.activation(out=lnd[:], in_=dd[:], func=ACT.Ln)
            lnr = seed.tile([P, 4], F32)
            nc.vector.tensor_scalar(out=lnr[:], in0=lnd[:], scalar1=1.0 / XPOS_BASE, scalar2=None, op0=ALU.mult)
            rr = seed.tile([P, 4, N], F32)
            for k in range(4):
                nc.scalar.activation(out=rr[:, k, :], in_=tt[:], func=ACT.Exp, scale=lnr[:, k : k + 1])

            sd = {}

            def seeds_phase(g):
                gs = slice(2 * g, 2 * g + 2)
                turns = seed.tile([P, 2, N], F32, name="turns%d" % g)
                nc.vector.scalar_tensor_tensor(
                    out=turns[:], in0=tt[:].unsqueeze(1).to_broadcast([P, 2, N]), scalar=1.0 / (2.0 * math.pi),
                    in1=ww[:, gs].unsqueeze(2).to_broadcast([P, 2, N]), op0=ALU.mult, op1=ALU.mult)
                whole = seed.tile([P, 2, N], I32, name="whole%d" % g)
                nc.vector.tensor_copy(out=whole[:], in_=turns[:])
                frac = seed.tile([P, 2, N], F32, name="frac%d" % g)
                nc.vector.tensor_tensor(out=frac[:], in0=turns[:], in1=whole[:], op=ALU.subtract)
                wrap = seed.tile([P, 2, N], F32, name="wrap%d" % g)
                nc.vector.scalar_tensor_tensor(out=wrap[:], in0=frac[:], scalar=0.25, in1=frac[:], op0=ALU.is_gt, op1=ALU.subtract)
                sd[g] = frac, wrap

            def seeds_sin(g):
                gs = slice(2 * g, 2 * g + 2)
                frac, wrap = sd[g]
                cs = seed.tile([P, 2, N], F32, name="cs%d" % g)
                nc.scalar.activation(out=cs[:], in_=wrap[:], func=ACT.Sin, scale=-2.0 * math.pi, bias=0.5 * math.pi)
                sn = seed.tile([P, 2, N], F32, name="sn%d" % g)
                nc.scalar.activation(out=sn[:], in_=frac[:], func=ACT.Sin, scale=2.0 * math.pi)
                for k, f in ((0, cs), (1, sn)):
                    nc.vector.tensor_tensor(out=zk[:, gs, k, :], in0=f[:, :, P:N], in1=rr[:, gs, P:N], op=ALU.mult)
                for k, f in ((0, cs), (1, sn)):
                    nc.vector.tensor_tensor(out=tab[:, gs, k, 0:P], in0=f[:, :, 0:P], in1=rr[:, gs, 0:P], op=ALU.mult)
                nc.vector.tensor_scalar(out=zk[:, gs, 2, :], in0=zk[:, gs, 1, :], scalar1=-1.0, scalar2=None, op0=ALU.mult)
                nc.vector.tensor_scalar(out=tab[:, gs, 2, 0:P], in0=tab[:, gs, 1, 0:P], scalar1=-1.0, scalar2=None, op0=ALU.mult)

            for what in LOADS:
                (load_g if what[0] == "g" else load_x if what[0] == "x" else load_w)(*what[1:])
            seeds_phase(0)
            seeds_phase(1)
            seeds_sin(0)
            seeds_sin(1)

        prod = ctx.enter_context(tc.tile_pool(name="prod", bufs=2))
        dpool = ctx.enter_context(tc.tile_pool(name="dpool", bufs=3))
        stage = ctx.enter_context(tc.tile_pool(name="stage", bufs=STAGE))

        tmps = {}

        def level_s(gu, k):
            src, dst, n = LEVELS[k]
            tmp = prod.tile([P, 2, 512], F32, tag="tmp", name="tmp", align_bytes=64, bufs=TMP)
            tmps[gu, k] = tmp
            for b in range(2):
                nc.scalar.activation(out=tmp[:, b, 0:n], in_=tab[:, gu, 1 - b, src : src + n], func=ACT.Copy, scale=zk[:, gu, 2 - b, k : k + 1])

        def level_v(gu, k):
            src, dst, n = LEVELS[k]
            nc.vector.scalar_tensor_tensor(
                out=tab[:, gu, 0:2, dst : dst + n], in0=tab[:, gu, 0:2, src : src + n], scalar=zk[:, gu, 0, k : k + 1],
                in1=tmps[gu, k][:, :, 0:n], op0=ALU.mult, op1=ALU.add)

        def level_n(gu, k):
            src, dst, n = LEVELS[k]
            nc.scalar.activation(out=tab[:, gu, 2, dst : dst + n], in_=tab[:, gu, 1, dst : dst + n], func=ACT.Copy, scale=-1.0)

        xc = keep.tile([P, 2, E], U32, align_bytes=64)
        xs = keep.tile([P, 2, E], U8, align_bytes=64)
        wc, ws, fc, fs = {}, {}, {}, {}
        for a in range(2):
            for g in range(2):
                for d, nm, dt in ((wc, "wc", U32), (ws, "ws", U8), (fc, "fc", U32), (fs, "fs", U8)):
                    t = keep.tile([P, 1024], dt, name="%s%d%d" % (nm, a, g), align_bytes=64)
                    d[a, g] = t
        kc, ks = {}, {}

        def tok_codes(f):
            if f not in kc:
                for d, nm, dt in ((kc, "kc", U32), (ks, "ks", U8)):
                    t = dpool.tile([P, 2, 512], dt, tag=nm, name=nm, align_bytes=64, bufs=KC)
                    d[f] = t
            return kc[f], ks[f]

        dfeat, dtok, gts, pqs = {}, {}, {}, {}

        def g_turn(k):
            a, g, r = CELLS[k]
            gt = psum.tile([P, 512], F32, tag="gt", name="gt")
            gts[k] = gt
            gw = graw[a, g, r][:].bitcast(F32)
            for u in range(2):
                for jx in range(2):
                    o = (2 * u + jx) * P
                    nc.tensor.transpose(gt[:, o : o + P], gw[:, jx, u : 256 : 2], ident[:])

        def gview(k):
            a, g, r = CELLS[k]
            c0 = 256 * r
            gv = gts[k][:].bitcast(BF16).rearrange("p (u k e) -> p k u e", u=2, e=2)
            return gv, tab[:, 2 * g : 2 * g + 2, :, c0 : c0 + 256].rearrange("p u c k -> p c k u")

        def prod_cos(k):
            gv, tb = gview(k)
            pp = prod.tile([P, 1024], F32, tag="pp", name="pp", align_bytes=64)
            qq = prod.tile([P, 1024], F32, tag="qq", name="qq", align_bytes=64)
            pqs[k] = pp, qq
            cb = tb[:, 0].unsqueeze(3).to_broadcast([P, 256, 2, 2])
            nc.vector.tensor_tensor(out=pp[:].rearrange("p (k u e) -> p k u e", u=2, e=2), in0=cb, in1=gv, op=ALU.mult)

        def prod_sin(k, lo, hi):
            gv, tb = gview(k)
            nc.vector.tensor_tensor(
                out=pqs[k][1][:, 4 * lo : 4 * hi].rearrange("p (k u e) -> p k u e", u=2, e=2), in0=tb[:, 1:3, lo:hi].rearrange("p e k u -> p k u e"),
                in1=gv[:, lo:hi, :, ::-1], op=ALU.mult)

        def add(k, engine, lo, hi):
            a, g, r = CELLS[k]
            i, h = (a, g, r // 2), r % 2
            if i not in dfeat:
                d = dpool.tile([P, 2048], BF16, tag="dfeat", name="dfeat", align_bytes=64, bufs=DFEAT)
                dfeat[i] = d
            pp, qq = pqs[k]
            o = 1024 * h
            engine.tensor_tensor(out=dfeat[i][:, o + 4 * lo : o + 4 * hi], in0=pp[:, 4 * lo : 4 * hi], in1=qq[:, 4 * lo : 4 * hi], op=ALU.add)

        def quant_feat(k):
            a, g, r = CELLS[k]
            cols = slice(256 * r, 256 * r + 256)
            o = 1024 * (r % 2)
            nc.vector.quantize_mx(out=fc[a, g][:, cols].bitcast(E5M2), scales=fs[a, g][:, cols], in_=dfeat[a, g, r // 2][:, o : o + 1024])

        def d_turn(i, u, eng="S"):
            if i not in dtok:
                d = dpool.tile([P, 2048], BF16, tag="dtok", name="dtok", align_bytes=64, bufs=2)
                dtok[i] = d
            dw = dfeat[i][:].bitcast(F32)
            dv = dtok[i][:].rearrange("q (p u r) -> q u p r", u=2, r=8)[:, u].rearrange("q p (e j) -> q p e j", j=4)
            dt = psum.tile([P, 512], F32, tag="dt", name="dt")
            for j in range(4):
                nc.tensor.transpose(dt[:, P * j : P * (j + 1)], dw[:, 256 * j + u : 256 * (j + 1) : 2], ident[:])
            cp = nc.scalar.copy if eng == "S" else nc.vector.tensor_copy
            cp(out=dv, in_=dt[:].bitcast(BF16).rearrange("q (j p e) -> q p e j", j=4, e=2))

        def quant_tok(i):
            a, g, tg = i
            codes, scales = tok_codes((a, g))
            nc.vector.quantize_mx(out=codes[:, tg].bitcast(E5M2), scales=scales[:, tg], in_=dtok[i][:])

        wide = {}

        def wide_tile(key):
            if key not in wide:
                t = dpool.tile([P, 2048], BF16, tag="wide", name="wide", align_bytes=64, bufs=3)
                wide[key] = t
            return wide[key]

        def x_lay(tg, h, eng):
            cp = nc.scalar.copy if eng == "S" else nc.vector.tensor_copy
            cp(out=wide_tile(("x", tg, h))[:].rearrange("p (e j) -> p e j", j=4), in_=xraw[tg][:, :, 512 * h : 512 * (h + 1)].rearrange("p j e -> p e j"))

        def x_quant(tg, h):
            cols = slice(512 * h, 512 * (h + 1))
            nc.vector.quantize_mx(out=xc[:, tg, cols].bitcast(E4M3), scales=xs[:, tg, cols], in_=wide["x", tg, h][:])

        def w_turn(a, h, g, b, eng):
            wv = wraw[a, h][:].bitcast(F32)
            ov = wide_tile((a, h, g))[:].bitcast(F32)
            wt = psum.tile([P, 512], F32, tag="acc", name="wt", bufs=4)
            for u in range(2):
                for k in range(2):
                    o = (2 * u + k) * P
                    nc.tensor.transpose(wt[:, o : o + P], wv[:, 2 * b + k, 256 * g + u : 256 * (g + 1) : 2], ident[:])
            cp = nc.scalar.copy if eng == "S" else nc.vector.tensor_copy
            cp(out=ov[:, 512 * b : 512 * (b + 1)].rearrange("p (n u) -> p n u", u=2), in_=wt[:].rearrange("p (u n) -> p n u", u=2))

        def w_quant(a, h, g):
            cols = slice(512 * h, 512 * (h + 1))
            nc.vector.quantize_mx(out=wc[a, g][:, cols].bitcast(E4M3), scales=ws[a, g][:, cols], in_=wide[a, h, g][:])

        def leave(acc, dst, eng):
            o = stage.tile([P, 512], F32, tag="o", name="o", align_bytes=64)
            cp = nc.scalar.copy if eng == "S" else nc.vector.tensor_copy
            cp(out=o[:], in_=acc[:])
            nc.sync.dma_start(out=dst, in_=o[:])

        def dw_mm(a, g, eb):
            acc = psum.tile([P, 512], F32, tag="acc", name="acc", bufs=4)
            m = slice(P * eb, P * (eb + 1))
            n = slice(512 * g, 512 * (g + 1))
            codes, scales = tok_codes((a, g))
            for tg in range(2):
                nc.tensor.matmul_mx(
                    out=acc[:], lhsT=xc[:, tg, m].bitcast(E4M3), lhsT_scale=xs[:, tg, m],
                    rhs=codes[:, tg].bitcast(E5M2), rhs_scale=scales[:, tg], start=(tg == 0), stop=(tg == 1))
            return acc, dw_hbm[a][m, n]

        def dx_mm(tg, j, h):
            acc = psum.tile([P, 512], F32, tag="acc", name="acc", bufs=4)
            m = slice(512 * tg + P * j, 512 * tg + P * (j + 1))
            n = slice(512 * h, 512 * (h + 1))
            for s, (a, g) in enumerate([(0, 0), (0, 1), (1, 0), (1, 1)]):
                nc.tensor.matmul_mx(
                    out=acc[:], lhsT=fc[a, g][:, m].bitcast(E5M2), lhsT_scale=fs[a, g][:, m],
                    rhs=wc[a, g][:, n].bitcast(E4M3), rhs_scale=ws[a, g][:, n], start=(s == 0), stop=(s == 3))
            return acc, dx_hbm[:, tg, j, n]

        V, G = nc.vector, nc.gpsimd
        NC = len(CELLS)
        at = CELLS.index
        w_units = [(a, h, g) for h in range(2) for a in range(2) for g in range(2)]
        x_units = [(tg, h) for tg in range(2) for h in range(2)]
        L = {k: [] for k in range(-1, NC + 2)}
        S_ = {k: [] for k in range(-1, NC + 2)}
        for gu, k, when in TABLE:
            if when >= 0:
                S_[when - 1].append((gu, k))
                L[when].append(lambda gu=gu, k=k: level_v(gu, k))
        for n, u in enumerate(x_units):
            L[XS + n + 1].append(lambda u=u: x_quant(*u))
        WAT = [WS + n for n in range(8)] if isinstance(WS, int) else WS
        for n, u in enumerate(w_units):
            L[WAT[n] + 1].append(lambda u=u: w_quant(*u))
        N_ = {k: [] for k in range(-1, NC + 2)}
        for gu, k, when in TABLE:
            if when >= 0:
                N_[when + 1].append((gu, k))
        turns, toks = {}, {}
        mx = []
        for a in range(2):
            for g in range(2):
                last = 0
                for tg in range(2):
                    kl = max(at((a, g, 2 * tg + h)) for h in range(2))
                    last = max(last, kl)
                    turns.setdefault(kl + 1, []).append((a, g, tg))
                    toks.setdefault(kl + 2, []).append((a, g, tg))
                mx.append((max(last + 2, XS + 6), 0, [(2, lambda a=a, g=g, e=e: dw_mm(a, g, e)) for e in range(8)]))
        for r in range(4):
            kr = max(at((a, g, r)) for a in range(2) for g in range(2))
            for h in range(2):
                ready = max(WAT[4 * h : 4 * h + 4]) + 2
                mx.append((max(kr + 2, ready), 1, [(4, lambda r=r, j=j, h=h: dx_mm(r // 2, 2 * (r % 2) + j, h)) for j in range(2)]))
        mx.sort(key=lambda m: (m[0], m[1]))
        mx = [(av, n, f) for av, kind, fs_ in mx for n, f in fs_]
        pend = []

        def groups(k, limit):
            n = 0
            while mx and mx[0][0] <= k and n + mx[0][1] <= limit:
                n += mx[0][1]
                if len(pend) == 3:
                    leave(*pend.pop(0), "S")
                pend.append(mx.pop(0)[2]())
            while pend:
                leave(*pend.pop(0), "S")

        g_turn(0)
        for gu, k, when in TABLE:
            if when < 0:
                level_s(gu, k)
                level_v(gu, k)
                level_n(gu, k)
        for gu, k in S_[-1]:
            level_s(gu, k)
        for k in range(NC):
            if k + 1 < NC:
                g_turn(k + 1)
            for gu, kk in N_[k]:
                level_n(gu, kk)
            if SFIRST:
                for gu, kk in S_[k]:
                    level_s(gu, kk)
            groups(k - 1, MXA)
            prod_cos(k)
            prod_sin(k, 0, QCUT)
            if k >= 1 and GTOK < 256 and k - 1 not in VK:
                add(k - 1, V, 0, 256 - GTOK)
            for c in toks.get(k, []):
                quant_tok(c)
            early = L[k][: (1 if EARLY else 0)] if not toks.get(k) else []
            for f in early:
                f()
            if k >= 1:
                quant_feat(k - 1)
            for c in turns.get(k, []):
                d_turn(c, 0)
                d_turn(c, 1)
            groups(k, MXB)
            for n in range(8):
                if WAT[n] == k:
                    a, h, g = w_units[n]
                    w_turn(a, h, g, 0, "S")
                    w_turn(a, h, g, 1, "S")
            if XS <= k < XS + 4:
                x_lay(*x_units[k - XS], "S")
            for f in L[k][len(early) :]:
                f()
            if not SFIRST:
                for gu, kk in S_[k]:
                    level_s(gu, kk)
            if QCUT < 256:
                prod_sin(k, QCUT, 256)
            if k in VK:
                add(k, V, 0, 256)
            elif GTOK > 0:
                add(k, G, 256 - GTOK, 256)
        if NC - 1 not in VK:
            add(NC - 1, V, 0, 256 - GTOK)
        quant_feat(NC - 1)
        for c in turns[NC]:
            d_turn(c, 0, "S")
            d_turn(c, 1, "V")
        cnt = 0
        last = [m for m in mx if m[0] > NC + 1]
        mx = [m for m in mx if m[0] <= NC + 1]
        for c in toks.get(NC, []):
            quant_tok(c)
        while mx or last:
            acc, dst = (mx or last).pop(0)[2]()
            leave(acc, dst, "SV"[cnt % 2])
            cnt += 1
            if cnt == 4:
                for c in toks[NC + 1]:
                    quant_tok(c)
